import numpy as np
import ml_dtypes


def mxq(x, axis, fmt="e4m3"):
    dtype, down = {"e4m3": (ml_dtypes.float8_e4m3fn, 7), "e5m2": (ml_dtypes.float8_e5m2, 14)}[fmt]
    v = np.moveaxis(np.asarray(x, np.float32).astype(ml_dtypes.bfloat16).astype(np.float64), axis, -1)
    blocks = v.reshape(v.shape[:-1] + (-1, 32))
    amax = np.abs(blocks).max(-1, keepdims=True)
    byte = np.maximum(np.where(amax > 0, np.frexp(amax)[1] - 1 + 127, 0) - down, 1)
    scale = np.exp2(byte - 127.0)
    codes = (blocks / scale).astype(np.float32).astype(dtype).astype(np.float64)
    return np.moveaxis((codes * scale).reshape(v.shape), -1, axis)


WIDE = False


def mx_kscale(k):
    if not WIDE:
        return np.ones(k)
    levels = np.array([10, -10, 5, -5, 0])
    a = np.random.permutation(np.resize(levels, k // 512 * 4)).reshape(k // 512, 4)
    idx = np.arange(k)
    return np.exp2(a[idx // 512, idx % 128 // 32])


BF16 = ml_dtypes.bfloat16


def bf(x):
    return np.asarray(x, np.float32).astype(BF16)


def f64(x):
    return np.asarray(x).astype(np.float64)


S, D, H, DH, F = 512, 1024, 8, 128, 4096
E = H * DH
EPS = 1e-5
XS = 0.015


def gelu_tanh(v):
    return 0.5 * v * (1.0 + np.tanh(np.sqrt(2.0 / np.pi) * (v + 0.044715 * v**3)))


def layernorm(x, scale, offset):
    mean = x.mean(axis=-1, keepdims=True)
    var = x.var(axis=-1, keepdims=True)
    return scale / np.sqrt(var + EPS) * (x - mean) + offset


def setup_inputs():
    s = mx_kscale(D)
    u = mx_kscale(E)
    x = np.random.standard_normal((S, D)) + 0.5 * np.random.standard_normal(S)[:, None]
    return {"x": bf(XS * x[None]),
            "attn_vec": bf(np.random.standard_normal((S, E)) * 0.6 * u),
            "ln_scale": bf((1.0 + 0.1 * np.random.standard_normal(D)) * s),
            "ln_offset": bf(0.1 * np.random.standard_normal(D) * s),
            "Wo": bf(np.random.standard_normal((E, D)) / np.sqrt(E) / u[:, None]),
            "W1": bf(np.random.standard_normal((D, F)) / np.sqrt(D) / s[:, None]),
            "b1": bf(0.1 * np.random.standard_normal(F)),
            "W2": bf(np.random.standard_normal((F, D)) / np.sqrt(F)),
            "b2": bf(0.1 * np.random.standard_normal(D))}


def reference(x, attn_vec, ln_scale, ln_offset, Wo, W1, b1, W2, b2):
    xn = layernorm(f64(x), f64(ln_scale), f64(ln_offset))
    attn_out = mxq(f64(attn_vec), 1, "e4m3") @ mxq(f64(Wo), 0, "e4m3")
    h = gelu_tanh((mxq(xn, 2, "e4m3") @ mxq(f64(W1), 0, "e4m3")) + f64(b1))
    dense_out = (mxq(h, 2, "e4m3") @ mxq(f64(W2), 0, "e4m3")) + f64(b2)
    return attn_out + dense_out

@@ -1,0 +1,321 @@
+from contextlib import ExitStack
+
+import concourse.mybir as mybir
+from concourse.masks import make_identity
+
+BF16 = mybir.dt.bfloat16
+F32 = mybir.dt.float32
+U32 = mybir.dt.uint32
+U8 = mybir.dt.uint8
+FP8X4 = mybir.dt.float8_e4m3fn_x4
+ACT = mybir.ActivationFunctionType
+ALU = mybir.AluOpType
+
+P = 128
+PACK = 4
+K_PASS = P * PACK
+BANK = 512
+
+TOKENS = 512
+D_MODEL = 1024
+D_FF = 4096
+EPS = 1e-5
+TOKEN_TILES = TOKENS // P
+D_PASSES = D_MODEL // K_PASS
+FF_PASSES = D_FF // K_PASS
+W1_COLS = 1024
+W1_RANGES = D_FF // W1_COLS
+
+VECTOR_SIXTEENTHS = 9
+
+B1_AT = 0
+LN_SCALE_AT = 32
+LN_OFFSET_AT = 64
+
+FLOPS = 2 * TOKENS * (D_MODEL * D_MODEL + 2 * D_MODEL * D_FF)
+
+
+def rows_128_apart(w, first_row, cols):
+    return [w[first_row : first_row + K_PASS, cols].rearrange("(t p) n -> p t n", p=P)]
+
+
+def rows_in_pairs(w, first_row, cols):
+    return [
+        w[first_row + 256 * u : first_row + 256 * (u + 1), cols].rearrange("(p e) n -> p e n", e=2)
+        for u in range(2)
+    ]
+
+
+def interleave(nc, grouped, raw, vector_cols):
+    width = raw.shape[2]
+    nc.vector.tensor_copy(
+        out=grouped[:, 0:vector_cols, :].rearrange("p (c i) t -> p c t i", i=4),
+        in_=raw[:, :, 0:vector_cols].rearrange("p t (c i) -> p c t i", i=4),
+    )
+    if vector_cols < width:
+        nc.scalar.copy(
+            out=grouped[:, vector_cols:width, :].rearrange("p (c i) t -> p c t i", i=4),
+            in_=raw[:, :, vector_cols:width].rearrange("p t (c i) -> p c t i", i=4),
+        )
+
+
+def quantise(nc, codes, scales, grouped):
+    nc.vector.quantize_mx(
+        out=codes.bitcast(FP8X4), scales=scales, in_=grouped.rearrange("p w t -> p (w t)")
+    )
+
+
+def quantise_weight_blocks(nc, pools, width, blocks_rows):
+    vector_cols = width * VECTOR_SIXTEENTHS // 16
+    staged = []
+    for pieces in blocks_rows:
+        raw = pools["raw"].tile([P, PACK, width], BF16)
+        rows_each = PACK // len(pieces)
+        for n, piece in enumerate(pieces):
+            nc.sync.dma_start(out=raw[:, n * rows_each : (n + 1) * rows_each, :], in_=piece)
+        grouped = pools["grouped"].tile([P, width, PACK], BF16, align_bytes=64)
+        interleave(nc, grouped, raw, vector_cols)
+        staged.append(grouped)
+    blocks = []
+    for grouped in staged:
+        codes = pools["codes"].tile([P, width], U32, align_bytes=64)
+        scales = pools["codes"].tile([P, width], U8, align_bytes=64)
+        quantise(nc, codes[:], scales[:], grouped[:])
+        blocks.append((codes, scales))
+    return blocks
+
+
+def add_pass_to_out(nc, acc, act_codes, act_scales, weight, start, stop):
+    w_codes, w_scales = weight
+    for i in range(TOKEN_TILES):
+        tokens = slice(i * P, (i + 1) * P)
+        nc.tensor.matmul_mx(
+            out=acc[i][:],
+            lhsT=act_codes[:, tokens].bitcast(FP8X4),
+            lhsT_scale=act_scales[:, tokens],
+            rhs=w_codes[:].bitcast(FP8X4),
+            rhs_scale=w_scales[:],
+            start=start,
+            stop=stop,
+        )
+
+
+def tile_transformerlayershard_pb_kernel(
+    tc, x, attn_vec, ln_scale, ln_offset, Wo, W1, b1, W2, b2, out
+):
+    nc = tc.nc
+    x_rows = x.rearrange("o s d -> (o s) d")
+    out_rows = out.rearrange("o s d -> (o s) d")
+
+    with ExitStack() as ctx:
+        const = ctx.enter_context(tc.tile_pool(name="const", bufs=1))
+        keep = ctx.enter_context(tc.tile_pool(name="keep", bufs=1))
+        w1_pools = {
+            "raw": ctx.enter_context(tc.tile_pool(name="w1_raw", bufs=3)),
+            "grouped": ctx.enter_context(tc.tile_pool(name="w1_grouped", bufs=4)),
+            "codes": ctx.enter_context(tc.tile_pool(name="w1_codes", bufs=4)),
+        }
+        acc_banks = ctx.enter_context(tc.psum_pool(name="acc_banks", bufs=4))
+        work_banks = ctx.enter_context(tc.psum_pool(name="work_banks", bufs=4))
+
+        xn_codes = keep.tile([P, D_PASSES, TOKENS], U32, align_bytes=64)
+        xn_scales = keep.tile([P, D_PASSES, TOKENS], U8, align_bytes=64)
+        attn_codes = keep.tile([P, D_PASSES, TOKENS], U32, align_bytes=64)
+        attn_scales = keep.tile([P, D_PASSES, TOKENS], U8, align_bytes=64)
+        h_codes = keep.tile([P, FF_PASSES, TOKENS], U32, align_bytes=64)
+        h_scales = keep.tile([P, FF_PASSES, TOKENS], U8, align_bytes=64)
+        b2_all = const.tile([P, D_MODEL], BF16)
+
+        def w1_blocks(r):
+            cols = slice(r * W1_COLS, (r + 1) * W1_COLS)
+            rows = [rows_128_apart(W1, c * K_PASS, cols) for c in range(D_PASSES)]
+            return quantise_weight_blocks(nc, w1_pools, W1_COLS, rows)
+
+        with tc.tile_pool(name="start", bufs=1) as start_pool:
+            x_sb = start_pool.tile([P, TOKEN_TILES, D_MODEL], BF16)
+            for i in range(TOKEN_TILES):
+                nc.sync.dma_start(out=x_sb[:, i, :], in_=x_rows[i * P : (i + 1) * P, :])
+
+            one = const.tile([P, 1], F32)
+            nc.vector.memset(one[:], 1.0)
+            table_warmer = const.tile([P, 1], F32)
+            nc.scalar.activation(out=table_warmer[:], in_=one[:], func=ACT.Sqrt)
+
+            ident_f32 = const.tile([P, P], F32)
+            make_identity(nc, ident_f32[:])
+            ident_bf16 = const.tile([P, P], BF16)
+            make_identity(nc, ident_bf16[:])
+
+            vec_rows = const.tile([P, P], BF16)
+            nc.vector.memset(vec_rows[:], 0.0)
+            for vec, at in ((b1, B1_AT), (ln_scale, LN_SCALE_AT), (ln_offset, LN_OFFSET_AT)):
+                rows = vec.rearrange("(r c) -> r c", c=P)
+                nc.sync.dma_start(out=vec_rows[at : at + rows.shape[0], :], in_=rows)
+            vec_bank = work_banks.tile([P, P], BF16, tag="work")
+            nc.tensor.transpose(vec_bank[:], vec_rows[:], ident_bf16[:])
+            vec_cols = const.tile([P, P], F32)
+            nc.vector.tensor_copy(out=vec_cols[:], in_=vec_bank[:])
+
+            stats = start_pool.tile([P, TOKEN_TILES, 2, 6], F32)
+            mean_var = start_pool.tile([P, TOKEN_TILES, 2], F32)
+            for i in range(TOKEN_TILES):
+                for half in range(2):
+                    nc.vector.bn_stats(
+                        out=stats[:, i, half, :], in_=x_sb[:, i, half * 512 : (half + 1) * 512]
+                    )
+                nc.vector.bn_aggr(
+                    out=mean_var[:, i, :], in_=stats[:, i, :, :].rearrange("p a b -> p (a b)")
+                )
+            var_eps = start_pool.tile([P, TOKEN_TILES], F32)
+            nc.vector.tensor_scalar(
+                out=var_eps[:], in0=mean_var[:, :, 1], scalar1=EPS, scalar2=None, op0=ALU.add
+            )
+            std = start_pool.tile([P, TOKEN_TILES], F32)
+            nc.scalar.activation(out=std[:], in_=var_eps[:], func=ACT.Sqrt)
+            rstd = start_pool.tile([P, TOKEN_TILES], F32)
+            nc.vector.reciprocal(out=rstd[:], in_=std[:])
+            z = start_pool.tile([P, TOKEN_TILES, D_MODEL], F32)
+            for i in range(TOKEN_TILES):
+                nc.vector.tensor_scalar(
+                    out=z[:, i, :],
+                    in0=x_sb[:, i, :],
+                    scalar1=mean_var[:, i, 0:1],
+                    scalar2=rstd[:, i : i + 1],
+                    op0=ALU.subtract,
+                    op1=ALU.mult,
+                )
+
+            xn_rows = start_pool.tile([P, D_PASSES, PACK, TOKENS], BF16)
+            xn_grouped = start_pool.tile([P, D_PASSES, TOKENS, PACK], BF16, align_bytes=64)
+            for c in range(D_PASSES):
+                for t in range(PACK):
+                    j = c * PACK + t
+                    z_bank = work_banks.tile([P, TOKENS], F32, tag="work")
+                    for i in range(TOKEN_TILES):
+                        nc.tensor.transpose(
+                            z_bank[:, i * P : (i + 1) * P], z[:, i, j * P : (j + 1) * P], ident_f32[:]
+                        )
+                    gain = vec_cols[:, LN_SCALE_AT + j : LN_SCALE_AT + j + 1]
+                    shift = vec_cols[:, LN_OFFSET_AT + j : LN_OFFSET_AT + j + 1]
+                    if t % 2 == 0:
+                        nc.scalar.activation(
+                            out=xn_rows[:, c, t, :], in_=z_bank[:], func=ACT.Identity, bias=shift, scale=gain
+                        )
+                    else:
+                        nc.vector.tensor_scalar(
+                            out=xn_rows[:, c, t, :],
+                            in0=z_bank[:],
+                            scalar1=gain,
+                            scalar2=shift,
+                            op0=ALU.mult,
+                            op1=ALU.add,
+                        )
+                interleave(nc, xn_grouped[:, c], xn_rows[:, c], TOKENS * VECTOR_SIXTEENTHS // 16)
+            for c in range(D_PASSES):
+                quantise(nc, xn_codes[:, c, :], xn_scales[:, c, :], xn_grouped[:, c])
+
+            w1_next = w1_blocks(0)
+
+            attn_sb = start_pool.tile([P, TOKEN_TILES * D_MODEL], BF16)
+            nc.sync.dma_start(
+                out=attn_sb[:].rearrange("p (i e) -> p i e", i=TOKEN_TILES),
+                in_=attn_vec.rearrange("(i p) e -> p i e", p=P),
+            )
+            attn_words = attn_sb[:].bitcast(F32).rearrange("p (i w) -> p i w", i=TOKEN_TILES)
+            attn_grouped = start_pool.tile([P, D_PASSES * TOKENS * PACK], BF16, align_bytes=64)
+            grouped_words = attn_grouped[:].bitcast(F32).rearrange("p (c s u) -> p c s u", c=D_PASSES, u=2)
+            for c in range(D_PASSES):
+                for pair in range(TOKEN_TILES // 2):
+                    attn_bank = work_banks.tile([P, 2, 2 * P], F32, tag="work")
+                    for u in range(2):
+                        for n in range(2):
+                            first_word = 256 * c + P * u
+                            nc.tensor.transpose(
+                                attn_bank[:, u, n * P : (n + 1) * P],
+                                attn_words[:, 2 * pair + n, first_word : first_word + P],
+                                ident_f32[:],
+                            )
+                    nc.scalar.copy(
+                        out=grouped_words[:, c, 2 * P * pair : 2 * P * (pair + 1), :],
+                        in_=attn_bank[:].rearrange("p u s -> p s u"),
+                    )
+            for c in range(D_PASSES):
+                nc.vector.quantize_mx(
+                    out=attn_codes[:, c, :].bitcast(FP8X4),
+                    scales=attn_scales[:, c, :],
+                    in_=attn_grouped[:, c * TOKENS * PACK : (c + 1) * TOKENS * PACK],
+                )
+
+        w2_pools = {
+            "raw": ctx.enter_context(tc.tile_pool(name="w2_raw", bufs=8, reuse_waits="tile")),
+            "grouped": ctx.enter_context(tc.tile_pool(name="w2_grouped", bufs=4, reuse_waits="tile")),
+            "codes": ctx.enter_context(tc.tile_pool(name="w2_codes", bufs=6, reuse_waits="tile")),
+        }
+        h_pool = ctx.enter_context(tc.tile_pool(name="h", bufs=2, reuse_waits="tile"))
+        out_pool = ctx.enter_context(tc.tile_pool(name="out", bufs=4, reuse_waits="tile"))
+
+        nc.sync.dma_start(out=b2_all[:], in_=b2.partition_broadcast(P))
+
+        def attention_product(acc, cols):
+            rows = [rows_in_pairs(Wo, c * K_PASS, cols) for c in range(D_PASSES)]
+            for c, weight in enumerate(quantise_weight_blocks(nc, w2_pools, BANK, rows)):
+                add_pass_to_out(nc, acc, attn_codes[:, c, :], attn_scales[:, c, :], weight, c == 0, False)
+
+        def second_product(acc, cols, passes):
+            rows = [rows_128_apart(W2, g * K_PASS, cols) for g in passes]
+            for g, weight in zip(passes, quantise_weight_blocks(nc, w2_pools, BANK, rows)):
+                add_pass_to_out(
+                    nc, acc, h_codes[:, g, :], h_scales[:, g, :], weight, False, g == FF_PASSES - 1
+                )
+
+        def add_b2_and_store(acc, cols):
+            for i in range(TOKEN_TILES):
+                result = out_pool.tile([P, BANK], F32)
+                nc.vector.tensor_tensor(out=result[:], in0=acc[i][:], in1=b2_all[:, cols], op=ALU.add)
+                nc.sync.dma_start(out=out_rows[i * P : (i + 1) * P, cols], in_=result[:])
+
+        def first_product(r, blocks):
+            for g in range(2 * r, 2 * r + 2):
+                h_rows = h_pool.tile([P, PACK, TOKENS], BF16)
+                for t in range(PACK):
+                    j = g * PACK + t
+                    cols = slice(j * P - r * W1_COLS, (j + 1) * P - r * W1_COLS)
+                    h_bank = work_banks.tile([P, TOKENS], F32, tag="work")
+                    for c, (codes, scales) in enumerate(blocks):
+                        nc.tensor.matmul_mx(
+                            out=h_bank[:],
+                            lhsT=codes[:, cols].bitcast(FP8X4),
+                            lhsT_scale=scales[:, cols],
+                            rhs=xn_codes[:, c, :].bitcast(FP8X4),
+                            rhs_scale=xn_scales[:, c, :],
+                            start=(c == 0),
+                            stop=(c == D_PASSES - 1),
+                        )
+                    nc.scalar.activation(
+                        out=h_rows[:, t, :],
+                        in_=h_bank[:],
+                        func=ACT.Gelu_apprx_tanh,
+                        bias=vec_cols[:, B1_AT + j : B1_AT + j + 1],
+                    )
+                h_grouped = h_pool.tile([P, TOKENS, PACK], BF16, align_bytes=64)
+                interleave(nc, h_grouped, h_rows, TOKENS)
+                quantise(nc, h_codes[:, g, :], h_scales[:, g, :], h_grouped[:])
+
+        first_cols = slice(0, BANK)
+        acc = [acc_banks.tile([P, BANK], F32, name="acc%d" % i, tag="acc") for i in range(TOKEN_TILES)]
+        for r in range(W1_RANGES):
+            w1_now = w1_next
+            if r + 1 < W1_RANGES:
+                w1_next = w1_blocks(r + 1)
+            first_product(r, w1_now)
+            if r == 0:
+                attention_product(acc, first_cols)
+            second_product(acc, first_cols, [2 * r, 2 * r + 1])
+        add_b2_and_store(acc, first_cols)
+
+        second_cols = slice(BANK, 2 * BANK)
+        acc = [work_banks.tile([P, BANK], F32, name="acc%d" % i, tag="work") for i in range(TOKEN_TILES)]
+        attention_product(acc, second_cols)
+        for g in range(0, FF_PASSES, 2):
+            second_product(acc, second_cols, [g, g + 1])
+        add_b2_and_store(acc, second_cols)

@@ -23,10 +23,17 @@ EPS = 1e-5
 TOKEN_TILES = TOKENS // P
 D_PASSES = D_MODEL // K_PASS
 FF_PASSES = D_FF // K_PASS
-W1_COLS = 1024
-W1_RANGES = D_FF // W1_COLS
 
-VECTOR_SIXTEENTHS = 9
+SECOND_LAG = 4
+
+INTERLEAVED_AHEAD = 6
+QUANTISED_AHEAD = 3
+RAW_BUFS = 10
+GROUPED_BUFS = INTERLEAVED_AHEAD - QUANTISED_AHEAD + 3
+CODES_BUFS = QUANTISED_AHEAD + 5
+
+VECTOR_COLS_BESIDE_GELU = 320
+VECTOR_COLS_AFTER_GELU = 224
 
 B1_AT = 0
 LN_SCALE_AT = 32
@@ -46,16 +53,16 @@ def rows_in_pairs(w, first_row, cols):
     ]
 
 
-def interleave(nc, grouped, raw, vector_cols):
-    width = raw.shape[2]
+def interleave(nc, grouped, rows, vector_cols):
+    width = rows.shape[2]
     nc.vector.tensor_copy(
         out=grouped[:, 0:vector_cols, :].rearrange("p (c i) t -> p c t i", i=4),
-        in_=raw[:, :, 0:vector_cols].rearrange("p t (c i) -> p c t i", i=4),
+        in_=rows[:, :, 0:vector_cols].rearrange("p t (c i) -> p c t i", i=4),
     )
     if vector_cols < width:
         nc.scalar.copy(
             out=grouped[:, vector_cols:width, :].rearrange("p (c i) t -> p c t i", i=4),
-            in_=raw[:, :, vector_cols:width].rearrange("p t (c i) -> p c t i", i=4),
+            in_=rows[:, :, vector_cols:width].rearrange("p t (c i) -> p c t i", i=4),
         )
 
 
@@ -63,26 +70,6 @@ def quantise(nc, codes, scales, grouped):
     nc.vector.quantize_mx(
         out=codes.bitcast(FP8X4), scales=scales, in_=grouped.rearrange("p w t -> p (w t)")
     )
-
-
-def quantise_weight_blocks(nc, pools, width, blocks_rows):
-    vector_cols = width * VECTOR_SIXTEENTHS // 16
-    staged = []
-    for pieces in blocks_rows:
-        raw = pools["raw"].tile([P, PACK, width], BF16)
-        rows_each = PACK // len(pieces)
-        for n, piece in enumerate(pieces):
-            nc.sync.dma_start(out=raw[:, n * rows_each : (n + 1) * rows_each, :], in_=piece)
-        grouped = pools["grouped"].tile([P, width, PACK], BF16, align_bytes=64)
-        interleave(nc, grouped, raw, vector_cols)
-        staged.append(grouped)
-    blocks = []
-    for grouped in staged:
-        codes = pools["codes"].tile([P, width], U32, align_bytes=64)
-        scales = pools["codes"].tile([P, width], U8, align_bytes=64)
-        quantise(nc, codes[:], scales[:], grouped[:])
-        blocks.append((codes, scales))
-    return blocks
 
 
 def add_pass_to_out(nc, acc, act_codes, act_scales, weight, start, stop):
@@ -106,15 +93,18 @@ def tile_transformerlayershard_pb_kernel(
     nc = tc.nc
     x_rows = x.rearrange("o s d -> (o s) d")
     out_rows = out.rearrange("o s d -> (o s) d")
+    halves = [slice(0, BANK), slice(BANK, 2 * BANK)]
 
     with ExitStack() as ctx:
+        ctx.enter_context(tc.manual_schedule())
         const = ctx.enter_context(tc.tile_pool(name="const", bufs=1))
         keep = ctx.enter_context(tc.tile_pool(name="keep", bufs=1))
-        w1_pools = {
-            "raw": ctx.enter_context(tc.tile_pool(name="w1_raw", bufs=3)),
-            "grouped": ctx.enter_context(tc.tile_pool(name="w1_grouped", bufs=4)),
-            "codes": ctx.enter_context(tc.tile_pool(name="w1_codes", bufs=4)),
-        }
+        start_pool = ctx.enter_context(tc.tile_pool(name="start", bufs=1))
+        raw_pool = ctx.enter_context(tc.tile_pool(name="raw", bufs=RAW_BUFS))
+        grouped_pool = ctx.enter_context(tc.tile_pool(name="grouped", bufs=GROUPED_BUFS))
+        codes_pool = ctx.enter_context(tc.tile_pool(name="codes", bufs=CODES_BUFS))
+        h_pool = ctx.enter_context(tc.tile_pool(name="h", bufs=2))
+        out_pool = ctx.enter_context(tc.tile_pool(name="out", bufs=2 * TOKEN_TILES))
         acc_banks = ctx.enter_context(tc.psum_pool(name="acc_banks", bufs=4))
         work_banks = ctx.enter_context(tc.psum_pool(name="work_banks", bufs=4))
 
@@ -124,198 +114,249 @@ def tile_transformerlayershard_pb_kernel(
         attn_scales = keep.tile([P, D_PASSES, TOKENS], U8, align_bytes=64)
         h_codes = keep.tile([P, FF_PASSES, TOKENS], U32, align_bytes=64)
         h_scales = keep.tile([P, FF_PASSES, TOKENS], U8, align_bytes=64)
+
+        blocks = []
+        for s in range(FF_PASSES + SECOND_LAG):
+            vector_cols = VECTOR_COLS_BESIDE_GELU if s < FF_PASSES else VECTOR_COLS_AFTER_GELU
+            if s < FF_PASSES:
+                for c in range(D_PASSES):
+                    blocks.append((rows_128_apart(W1, c * K_PASS, slice(s * BANK, (s + 1) * BANK)), vector_cols))
+            if s == SECOND_LAG:
+                for c in range(D_PASSES):
+                    blocks.append((rows_in_pairs(Wo, c * K_PASS, halves[0]), vector_cols))
+            if s >= SECOND_LAG:
+                blocks.append((rows_128_apart(W2, (s - SECOND_LAG) * K_PASS, halves[0]), vector_cols))
+        for c in range(D_PASSES):
+            blocks.append((rows_in_pairs(Wo, c * K_PASS, halves[1]), VECTOR_COLS_AFTER_GELU))
+        for g in range(FF_PASSES):
+            blocks.append((rows_128_apart(W2, g * K_PASS, halves[1]), VECTOR_COLS_AFTER_GELU))
+
+        loaded = []
+        interleaved = []
+        quantised = []
+        used = []
+
+        def load_next():
+            if len(loaded) < len(blocks):
+                pieces = blocks[len(loaded)][0]
+                raw = raw_pool.tile([P, PACK, BANK], BF16)
+                rows_each = PACK // len(pieces)
+                for n, piece in enumerate(pieces):
+                    nc.sync.dma_start(out=raw[:, n * rows_each : (n + 1) * rows_each, :], in_=piece)
+                loaded.append(raw)
+
+        def interleave_next():
+            if len(interleaved) < len(blocks):
+                n = len(interleaved)
+                grouped = grouped_pool.tile([P, BANK, PACK], BF16, align_bytes=64)
+                interleave(nc, grouped, loaded[n], blocks[n][1])
+                interleaved.append(grouped)
+                load_next()
+
+        def quantise_next():
+            if len(quantised) < len(blocks):
+                codes = codes_pool.tile([P, BANK], U32, align_bytes=64)
+                scales = codes_pool.tile([P, BANK], U8, align_bytes=64)
+                quantise(nc, codes[:], scales[:], interleaved[len(quantised)][:])
+                quantised.append((codes, scales))
+
+        def prepare_next():
+            interleave_next()
+            quantise_next()
+
+        def next_block():
+            used.append(quantised[len(used)])
+            return used[len(used) - 1]
+
+        one = const.tile([P, 1], F32)
+        nc.vector.memset(one[:], 1.0)
+        vec_rows = const.tile([P, P], BF16)
+        nc.vector.memset(vec_rows[:], 0.0)
+        table_warmer = const.tile([P, 1], F32)
+        nc.scalar.activation(out=table_warmer[:], in_=one[:], func=ACT.Sqrt)
+        ident_f32 = const.tile([P, P], F32)
+        make_identity(nc, ident_f32[:])
+        ident_bf16 = const.tile([P, P], BF16)
+        make_identity(nc, ident_bf16[:])
+
+        x_sb = start_pool.tile([P, TOKEN_TILES, D_MODEL], BF16)
+        for i in range(TOKEN_TILES):
+            nc.sync.dma_start(out=x_sb[:, i, :], in_=x_rows[i * P : (i + 1) * P, :])
+        load_next()
+        load_next()
+        for vec, at in ((b1, B1_AT), (ln_scale, LN_SCALE_AT), (ln_offset, LN_OFFSET_AT)):
+            rows = vec.rearrange("(r c) -> r c", c=P)
+            nc.sync.dma_start(out=vec_rows[at : at + rows.shape[0], :], in_=rows)
+        load_next()
+        load_next()
+        attn_sb = start_pool.tile([P, TOKEN_TILES * D_MODEL], BF16)
+        nc.sync.dma_start(
+            out=attn_sb[:].rearrange("p (i e) -> p i e", i=TOKEN_TILES),
+            in_=attn_vec.rearrange("(i p) e -> p i e", p=P),
+        )
+        for n in range(RAW_BUFS - 4):
+            load_next()
         b2_all = const.tile([P, D_MODEL], BF16)
-
-        def w1_blocks(r):
-            cols = slice(r * W1_COLS, (r + 1) * W1_COLS)
-            rows = [rows_128_apart(W1, c * K_PASS, cols) for c in range(D_PASSES)]
-            return quantise_weight_blocks(nc, w1_pools, W1_COLS, rows)
-
-        with tc.tile_pool(name="start", bufs=1) as start_pool:
-            x_sb = start_pool.tile([P, TOKEN_TILES, D_MODEL], BF16)
-            for i in range(TOKEN_TILES):
-                nc.sync.dma_start(out=x_sb[:, i, :], in_=x_rows[i * P : (i + 1) * P, :])
-
-            one = const.tile([P, 1], F32)
-            nc.vector.memset(one[:], 1.0)
-            table_warmer = const.tile([P, 1], F32)
-            nc.scalar.activation(out=table_warmer[:], in_=one[:], func=ACT.Sqrt)
-
-            ident_f32 = const.tile([P, P], F32)
-            make_identity(nc, ident_f32[:])
-            ident_bf16 = const.tile([P, P], BF16)
-            make_identity(nc, ident_bf16[:])
-
-            vec_rows = const.tile([P, P], BF16)
-            nc.vector.memset(vec_rows[:], 0.0)
-            for vec, at in ((b1, B1_AT), (ln_scale, LN_SCALE_AT), (ln_offset, LN_OFFSET_AT)):
-                rows = vec.rearrange("(r c) -> r c", c=P)
-                nc.sync.dma_start(out=vec_rows[at : at + rows.shape[0], :], in_=rows)
-            vec_bank = work_banks.tile([P, P], BF16, tag="work")
-            nc.tensor.transpose(vec_bank[:], vec_rows[:], ident_bf16[:])
-            vec_cols = const.tile([P, P], F32)
-            nc.vector.tensor_copy(out=vec_cols[:], in_=vec_bank[:])
-
-            stats = start_pool.tile([P, TOKEN_TILES, 2, 6], F32)
-            mean_var = start_pool.tile([P, TOKEN_TILES, 2], F32)
-            for i in range(TOKEN_TILES):
-                for half in range(2):
-                    nc.vector.bn_stats(
-                        out=stats[:, i, half, :], in_=x_sb[:, i, half * 512 : (half + 1) * 512]
-                    )
-                nc.vector.bn_aggr(
-                    out=mean_var[:, i, :], in_=stats[:, i, :, :].rearrange("p a b -> p (a b)")
-                )
-            var_eps = start_pool.tile([P, TOKEN_TILES], F32)
-            nc.vector.tensor_scalar(
-                out=var_eps[:], in0=mean_var[:, :, 1], scalar1=EPS, scalar2=None, op0=ALU.add
-            )
-            std = start_pool.tile([P, TOKEN_TILES], F32)
-            nc.scalar.activation(out=std[:], in_=var_eps[:], func=ACT.Sqrt)
-            rstd = start_pool.tile([P, TOKEN_TILES], F32)
-            nc.vector.reciprocal(out=rstd[:], in_=std[:])
-            z = start_pool.tile([P, TOKEN_TILES, D_MODEL], F32)
-            for i in range(TOKEN_TILES):
-                nc.vector.tensor_scalar(
-                    out=z[:, i, :],
-                    in0=x_sb[:, i, :],
-                    scalar1=mean_var[:, i, 0:1],
-                    scalar2=rstd[:, i : i + 1],
-                    op0=ALU.subtract,
-                    op1=ALU.mult,
-                )
-
-            xn_rows = start_pool.tile([P, D_PASSES, PACK, TOKENS], BF16)
-            xn_grouped = start_pool.tile([P, D_PASSES, TOKENS, PACK], BF16, align_bytes=64)
-            for c in range(D_PASSES):
-                for t in range(PACK):
-                    j = c * PACK + t
-                    z_bank = work_banks.tile([P, TOKENS], F32, tag="work")
-                    for i in range(TOKEN_TILES):
-                        nc.tensor.transpose(
-                            z_bank[:, i * P : (i + 1) * P], z[:, i, j * P : (j + 1) * P], ident_f32[:]
-                        )
-                    gain = vec_cols[:, LN_SCALE_AT + j : LN_SCALE_AT + j + 1]
-                    shift = vec_cols[:, LN_OFFSET_AT + j : LN_OFFSET_AT + j + 1]
-                    if t % 2 == 0:
-                        nc.scalar.activation(
-                            out=xn_rows[:, c, t, :], in_=z_bank[:], func=ACT.Identity, bias=shift, scale=gain
-                        )
-                    else:
-                        nc.vector.tensor_scalar(
-                            out=xn_rows[:, c, t, :],
-                            in0=z_bank[:],
-                            scalar1=gain,
-                            scalar2=shift,
-                            op0=ALU.mult,
-                            op1=ALU.add,
-                        )
-                interleave(nc, xn_grouped[:, c], xn_rows[:, c], TOKENS * VECTOR_SIXTEENTHS // 16)
-            for c in range(D_PASSES):
-                quantise(nc, xn_codes[:, c, :], xn_scales[:, c, :], xn_grouped[:, c])
-
-            w1_next = w1_blocks(0)
-
-            attn_sb = start_pool.tile([P, TOKEN_TILES * D_MODEL], BF16)
-            nc.sync.dma_start(
-                out=attn_sb[:].rearrange("p (i e) -> p i e", i=TOKEN_TILES),
-                in_=attn_vec.rearrange("(i p) e -> p i e", p=P),
-            )
-            attn_words = attn_sb[:].bitcast(F32).rearrange("p (i w) -> p i w", i=TOKEN_TILES)
-            attn_grouped = start_pool.tile([P, D_PASSES * TOKENS * PACK], BF16, align_bytes=64)
-            grouped_words = attn_grouped[:].bitcast(F32).rearrange("p (c s u) -> p c s u", c=D_PASSES, u=2)
-            for c in range(D_PASSES):
-                for pair in range(TOKEN_TILES // 2):
-                    attn_bank = work_banks.tile([P, 2, 2 * P], F32, tag="work")
-                    for u in range(2):
-                        for n in range(2):
-                            first_word = 256 * c + P * u
-                            nc.tensor.transpose(
-                                attn_bank[:, u, n * P : (n + 1) * P],
-                                attn_words[:, 2 * pair + n, first_word : first_word + P],
-                                ident_f32[:],
-                            )
-                    nc.scalar.copy(
-                        out=grouped_words[:, c, 2 * P * pair : 2 * P * (pair + 1), :],
-                        in_=attn_bank[:].rearrange("p u s -> p s u"),
-                    )
-            for c in range(D_PASSES):
-                nc.vector.quantize_mx(
-                    out=attn_codes[:, c, :].bitcast(FP8X4),
-                    scales=attn_scales[:, c, :],
-                    in_=attn_grouped[:, c * TOKENS * PACK : (c + 1) * TOKENS * PACK],
-                )
-
-        w2_pools = {
-            "raw": ctx.enter_context(tc.tile_pool(name="w2_raw", bufs=8, reuse_waits="tile")),
-            "grouped": ctx.enter_context(tc.tile_pool(name="w2_grouped", bufs=4, reuse_waits="tile")),
-            "codes": ctx.enter_context(tc.tile_pool(name="w2_codes", bufs=6, reuse_waits="tile")),
-        }
-        h_pool = ctx.enter_context(tc.tile_pool(name="h", bufs=2, reuse_waits="tile"))
-        out_pool = ctx.enter_context(tc.tile_pool(name="out", bufs=4, reuse_waits="tile"))
-
         nc.sync.dma_start(out=b2_all[:], in_=b2.partition_broadcast(P))
 
-        def attention_product(acc, cols):
-            rows = [rows_in_pairs(Wo, c * K_PASS, cols) for c in range(D_PASSES)]
-            for c, weight in enumerate(quantise_weight_blocks(nc, w2_pools, BANK, rows)):
-                add_pass_to_out(nc, acc, attn_codes[:, c, :], attn_scales[:, c, :], weight, c == 0, False)
+        stats = start_pool.tile([P, TOKEN_TILES, 2, 6], F32)
+        mean_var = start_pool.tile([P, TOKEN_TILES, 2], F32)
+        for i in range(TOKEN_TILES):
+            for half in range(2):
+                nc.vector.bn_stats(out=stats[:, i, half, :], in_=x_sb[:, i, half * 512 : (half + 1) * 512])
+            nc.vector.bn_aggr(out=mean_var[:, i, :], in_=stats[:, i, :, :].rearrange("p a b -> p (a b)"))
+        var_eps = start_pool.tile([P, TOKEN_TILES], F32)
+        nc.vector.tensor_scalar(out=var_eps[:], in0=mean_var[:, :, 1], scalar1=EPS, scalar2=None, op0=ALU.add)
 
-        def second_product(acc, cols, passes):
-            rows = [rows_128_apart(W2, g * K_PASS, cols) for g in passes]
-            for g, weight in zip(passes, quantise_weight_blocks(nc, w2_pools, BANK, rows)):
-                add_pass_to_out(
-                    nc, acc, h_codes[:, g, :], h_scales[:, g, :], weight, False, g == FF_PASSES - 1
+        vec_bank = work_banks.tile([P, P], BF16, tag="work")
+        nc.tensor.transpose(vec_bank[:], vec_rows[:], ident_bf16[:])
+        vec_cols = const.tile([P, P], F32)
+        nc.vector.tensor_copy(out=vec_cols[:], in_=vec_bank[:])
+
+        interleave_next()
+        interleave_next()
+        std = start_pool.tile([P, TOKEN_TILES], F32)
+        nc.scalar.activation(out=std[:], in_=var_eps[:], func=ACT.Sqrt)
+        rstd = start_pool.tile([P, TOKEN_TILES], F32)
+        nc.vector.reciprocal(out=rstd[:], in_=std[:])
+        minus_mean_rstd = start_pool.tile([P, TOKEN_TILES], F32)
+        nc.vector.scalar_tensor_tensor(
+            out=minus_mean_rstd[:], in0=mean_var[:, :, 0], scalar=-1.0, in1=rstd[:], op0=ALU.mult, op1=ALU.mult
+        )
+        interleave_next()
+        z = start_pool.tile([P, TOKEN_TILES, D_MODEL], F32)
+        for i in range(TOKEN_TILES):
+            gain = rstd[:, i : i + 1]
+            shift = minus_mean_rstd[:, i : i + 1]
+            if i % 2 == 0:
+                nc.scalar.activation(out=z[:, i, :], in_=x_sb[:, i, :], func=ACT.Identity, bias=shift, scale=gain)
+            else:
+                nc.vector.tensor_scalar(
+                    out=z[:, i, :], in0=x_sb[:, i, :], scalar1=gain, scalar2=shift, op0=ALU.mult, op1=ALU.add
                 )
+        interleave_next()
+        quantise_next()
+        quantise_next()
 
-        def add_b2_and_store(acc, cols):
-            for i in range(TOKEN_TILES):
-                result = out_pool.tile([P, BANK], F32)
-                nc.vector.tensor_tensor(out=result[:], in0=acc[i][:], in1=b2_all[:, cols], op=ALU.add)
-                nc.sync.dma_start(out=out_rows[i * P : (i + 1) * P, cols], in_=result[:])
-
-        def first_product(r, blocks):
-            for g in range(2 * r, 2 * r + 2):
-                h_rows = h_pool.tile([P, PACK, TOKENS], BF16)
-                for t in range(PACK):
-                    j = g * PACK + t
-                    cols = slice(j * P - r * W1_COLS, (j + 1) * P - r * W1_COLS)
-                    h_bank = work_banks.tile([P, TOKENS], F32, tag="work")
-                    for c, (codes, scales) in enumerate(blocks):
-                        nc.tensor.matmul_mx(
-                            out=h_bank[:],
-                            lhsT=codes[:, cols].bitcast(FP8X4),
-                            lhsT_scale=scales[:, cols],
-                            rhs=xn_codes[:, c, :].bitcast(FP8X4),
-                            rhs_scale=xn_scales[:, c, :],
-                            start=(c == 0),
-                            stop=(c == D_PASSES - 1),
-                        )
-                    nc.scalar.activation(
-                        out=h_rows[:, t, :],
-                        in_=h_bank[:],
-                        func=ACT.Gelu_apprx_tanh,
-                        bias=vec_cols[:, B1_AT + j : B1_AT + j + 1],
+        xn_rows = start_pool.tile([P, D_PASSES, PACK, TOKENS], BF16)
+        xn_grouped = start_pool.tile([P, D_PASSES, TOKENS, PACK], BF16, align_bytes=64)
+        for c in range(D_PASSES):
+            for t in range(PACK):
+                j = c * PACK + t
+                if c == 0:
+                    z_bank = work_banks.tile([P, TOKENS], F32, tag="work")
+                else:
+                    z_bank = acc_banks.tile([P, TOKENS], F32, tag="acc")
+                for i in range(TOKEN_TILES):
+                    nc.tensor.transpose(z_bank[:, i * P : (i + 1) * P], z[:, i, j * P : (j + 1) * P], ident_f32[:])
+                gain = vec_cols[:, LN_SCALE_AT + j : LN_SCALE_AT + j + 1]
+                shift = vec_cols[:, LN_OFFSET_AT + j : LN_OFFSET_AT + j + 1]
+                if t % 2 == 0:
+                    nc.scalar.activation(out=xn_rows[:, c, t, :], in_=z_bank[:], func=ACT.Identity, bias=shift, scale=gain)
+                else:
+                    nc.vector.tensor_scalar(
+                        out=xn_rows[:, c, t, :], in0=z_bank[:], scalar1=gain, scalar2=shift, op0=ALU.mult, op1=ALU.add
                     )
+            interleave(nc, xn_grouped[:, c], xn_rows[:, c], VECTOR_COLS_BESIDE_GELU)
+        quantise_next()
+        for c in range(D_PASSES):
+            quantise(nc, xn_codes[:, c, :], xn_scales[:, c, :], xn_grouped[:, c])
+
+        attn_words = attn_sb[:].bitcast(F32).rearrange("p (i w) -> p i w", i=TOKEN_TILES)
+        attn_grouped = start_pool.tile([P, D_PASSES * TOKENS * PACK], BF16, align_bytes=64)
+        grouped_words = attn_grouped[:].bitcast(F32).rearrange("p (c s u) -> p c s u", c=D_PASSES, u=2)
+        for c in range(D_PASSES):
+            for pair in range(TOKEN_TILES // 2):
+                attn_bank = work_banks.tile([P, 2, 2 * P], F32, tag="work")
+                for u in range(2):
+                    for n in range(2):
+                        first_word = 256 * c + P * u
+                        nc.tensor.transpose(
+                            attn_bank[:, u, n * P : (n + 1) * P],
+                            attn_words[:, 2 * pair + n, first_word : first_word + P],
+                            ident_f32[:],
+                        )
+                nc.scalar.copy(
+                    out=grouped_words[:, c, 2 * P * pair : 2 * P * (pair + 1), :],
+                    in_=attn_bank[:].rearrange("p u s -> p s u"),
+                )
+        while len(interleaved) < INTERLEAVED_AHEAD:
+            interleave_next()
+        for c in range(D_PASSES):
+            nc.vector.quantize_mx(
+                out=attn_codes[:, c, :].bitcast(FP8X4),
+                scales=attn_scales[:, c, :],
+                in_=attn_grouped[:, c * TOKENS * PACK : (c + 1) * TOKENS * PACK],
+            )
+        while len(quantised) < QUANTISED_AHEAD:
+            quantise_next()
+
+        def first_product(g):
+            w1 = [next_block() for c in range(D_PASSES)]
+            h_rows = h_pool.tile([P, PACK, TOKENS], BF16)
+            for t in range(PACK):
+                cols = slice(t * P, (t + 1) * P)
+                h_bank = work_banks.tile([P, TOKENS], F32, tag="work")
+                for c, (codes, scales) in enumerate(w1):
+                    nc.tensor.matmul_mx(
+                        out=h_bank[:],
+                        lhsT=codes[:, cols].bitcast(FP8X4),
+                        lhsT_scale=scales[:, cols],
+                        rhs=xn_codes[:, c, :].bitcast(FP8X4),
+                        rhs_scale=xn_scales[:, c, :],
+                        start=(c == 0),
+                        stop=(c == D_PASSES - 1),
+                    )
+                j = g * PACK + t
+                nc.scalar.activation(
+                    out=h_rows[:, t, :],
+                    in_=h_bank[:],
+                    func=ACT.Gelu_apprx_tanh,
+                    bias=vec_cols[:, B1_AT + j : B1_AT + j + 1],
+                )
+            return h_rows
+
+        def attention_pass(acc, c):
+            add_pass_to_out(nc, acc, attn_codes[:, c, :], attn_scales[:, c, :], next_block(), c == 0, False)
+
+        def second_product(acc, g):
+            add_pass_to_out(nc, acc, h_codes[:, g, :], h_scales[:, g, :], next_block(), False, g == FF_PASSES - 1)
+
+        def add_b2_and_store(acc, i, cols):
+            result = out_pool.tile([P, BANK], F32)
+            nc.vector.tensor_tensor(out=result[:], in0=acc[i][:], in1=b2_all[:, cols], op=ALU.add)
+            nc.sync.dma_start(out=out_rows[i * P : (i + 1) * P, cols], in_=result[:])
+
+        first_acc = [acc_banks.tile([P, BANK], F32, name="acc%d" % i, tag="acc") for i in range(TOKEN_TILES)]
+        h_rows_of = {}
+        for s in range(FF_PASSES + SECOND_LAG):
+            g = s - 1
+            if g in h_rows_of:
                 h_grouped = h_pool.tile([P, TOKENS, PACK], BF16, align_bytes=64)
-                interleave(nc, h_grouped, h_rows, TOKENS)
+                interleave(nc, h_grouped, h_rows_of[g], TOKENS)
+            if s < FF_PASSES:
+                h_rows_of[s] = first_product(s)
+                for c in range(D_PASSES):
+                    prepare_next()
+            if s == SECOND_LAG:
+                for c in range(D_PASSES):
+                    attention_pass(first_acc, c)
+                    prepare_next()
+            if s >= SECOND_LAG:
+                second_product(first_acc, s - SECOND_LAG)
+                prepare_next()
+            if g in h_rows_of:
                 quantise(nc, h_codes[:, g, :], h_scales[:, g, :], h_grouped[:])
 
-        first_cols = slice(0, BANK)
-        acc = [acc_banks.tile([P, BANK], F32, name="acc%d" % i, tag="acc") for i in range(TOKEN_TILES)]
-        for r in range(W1_RANGES):
-            w1_now = w1_next
-            if r + 1 < W1_RANGES:
-                w1_next = w1_blocks(r + 1)
-            first_product(r, w1_now)
-            if r == 0:
-                attention_product(acc, first_cols)
-            second_product(acc, first_cols, [2 * r, 2 * r + 1])
-        add_b2_and_store(acc, first_cols)
-
-        second_cols = slice(BANK, 2 * BANK)
-        acc = [work_banks.tile([P, BANK], F32, name="acc%d" % i, tag="work") for i in range(TOKEN_TILES)]
-        attention_product(acc, second_cols)
-        for g in range(0, FF_PASSES, 2):
-            second_product(acc, second_cols, [g, g + 1])
-        add_b2_and_store(acc, second_cols)
+        second_acc = [work_banks.tile([P, BANK], F32, name="acc%d" % i, tag="work") for i in range(TOKEN_TILES)]
+        rounds = D_PASSES + FF_PASSES
+        for n in range(rounds):
+            if n < D_PASSES:
+                attention_pass(second_acc, n)
+            else:
+                second_product(second_acc, n - D_PASSES)
+            prepare_next()
+            if n >= rounds - TOKEN_TILES:
+                add_b2_and_store(first_acc, n - (rounds - TOKEN_TILES), halves[0])
+        for i in range(TOKEN_TILES):
+            add_b2_and_store(second_acc, i, halves[1])

@@ -96,7 +96,6 @@ def tile_transformerlayershard_pb_kernel(
     halves = [slice(0, BANK), slice(BANK, 2 * BANK)]
 
     with ExitStack() as ctx:
-        ctx.enter_context(tc.manual_schedule())
         const = ctx.enter_context(tc.tile_pool(name="const", bufs=1))
         keep = ctx.enter_context(tc.tile_pool(name="keep", bufs=1))
         start_pool = ctx.enter_context(tc.tile_pool(name="start", bufs=1))

@@ -15,6 +15,9 @@ P = 128
 PACK = 4
 K_PASS = P * PACK
 BANK = 512
+BANKS = 8
+BN_STATS_MAX = 512
+BN_STATS_OUT = 6
 
 TOKENS = 512
 D_MODEL = 1024
@@ -48,7 +51,7 @@ def rows_128_apart(w, first_row, cols):
 
 def rows_in_pairs(w, first_row, cols):
     return [
-        w[first_row + 256 * u : first_row + 256 * (u + 1), cols].rearrange("(p e) n -> p e n", e=2)
+        w[first_row + 2 * P * u : first_row + 2 * P * (u + 1), cols].rearrange("(p e) n -> p e n", e=2)
         for u in range(2)
     ]
 
@@ -104,8 +107,8 @@ def tile_transformerlayershard_pb_kernel(
         codes_pool = ctx.enter_context(tc.tile_pool(name="codes", bufs=CODES_BUFS))
         h_pool = ctx.enter_context(tc.tile_pool(name="h", bufs=2))
         out_pool = ctx.enter_context(tc.tile_pool(name="out", bufs=2 * TOKEN_TILES))
-        acc_banks = ctx.enter_context(tc.psum_pool(name="acc_banks", bufs=4))
-        work_banks = ctx.enter_context(tc.psum_pool(name="work_banks", bufs=4))
+        acc_banks = ctx.enter_context(tc.psum_pool(name="acc_banks", bufs=BANKS // 2))
+        work_banks = ctx.enter_context(tc.psum_pool(name="work_banks", bufs=BANKS // 2))
 
         xn_codes = keep.tile([P, D_PASSES, TOKENS], U32, align_bytes=64)
         xn_scales = keep.tile([P, D_PASSES, TOKENS], U8, align_bytes=64)
@@ -140,8 +143,8 @@ def tile_transformerlayershard_pb_kernel(
                 pieces = blocks[len(loaded)][0]
                 raw = raw_pool.tile([P, PACK, BANK], BF16)
                 rows_each = PACK // len(pieces)
-                for n, piece in enumerate(pieces):
-                    nc.sync.dma_start(out=raw[:, n * rows_each : (n + 1) * rows_each, :], in_=piece)
+                for k, piece in enumerate(pieces):
+                    nc.sync.dma_start(out=raw[:, k * rows_each : (k + 1) * rows_each, :], in_=piece)
                 loaded.append(raw)
 
         def interleave_next():
@@ -181,39 +184,38 @@ def tile_transformerlayershard_pb_kernel(
         x_sb = start_pool.tile([P, TOKEN_TILES, D_MODEL], BF16)
         for i in range(TOKEN_TILES):
             nc.sync.dma_start(out=x_sb[:, i, :], in_=x_rows[i * P : (i + 1) * P, :])
-        load_next()
-        load_next()
+        for c in range(D_PASSES):
+            load_next()
         for vec, at in ((b1, B1_AT), (ln_scale, LN_SCALE_AT), (ln_offset, LN_OFFSET_AT)):
-            rows = vec.rearrange("(r c) -> r c", c=P)
-            nc.sync.dma_start(out=vec_rows[at : at + rows.shape[0], :], in_=rows)
-        load_next()
-        load_next()
+            vec_as_rows = vec.rearrange("(r c) -> r c", c=P)
+            nc.sync.dma_start(out=vec_rows[at : at + vec_as_rows.shape[0], :], in_=vec_as_rows)
+        for c in range(D_PASSES):
+            load_next()
         attn_sb = start_pool.tile([P, TOKEN_TILES * D_MODEL], BF16)
         nc.sync.dma_start(
             out=attn_sb[:].rearrange("p (i e) -> p i e", i=TOKEN_TILES),
             in_=attn_vec.rearrange("(i p) e -> p i e", p=P),
         )
-        for n in range(RAW_BUFS - 4):
+        while len(loaded) < RAW_BUFS:
             load_next()
         b2_all = const.tile([P, D_MODEL], BF16)
         nc.sync.dma_start(out=b2_all[:], in_=b2.partition_broadcast(P))
-
-        stats = start_pool.tile([P, TOKEN_TILES, 2, 6], F32)
-        mean_var = start_pool.tile([P, TOKEN_TILES, 2], F32)
-        for i in range(TOKEN_TILES):
-            for half in range(2):
-                nc.vector.bn_stats(out=stats[:, i, half, :], in_=x_sb[:, i, half * 512 : (half + 1) * 512])
-            nc.vector.bn_aggr(out=mean_var[:, i, :], in_=stats[:, i, :, :].rearrange("p a b -> p (a b)"))
-        var_eps = start_pool.tile([P, TOKEN_TILES], F32)
-        nc.vector.tensor_scalar(out=var_eps[:], in0=mean_var[:, :, 1], scalar1=EPS, scalar2=None, op0=ALU.add)
 
         vec_bank = work_banks.tile([P, P], BF16, tag="work")
         nc.tensor.transpose(vec_bank[:], vec_rows[:], ident_bf16[:])
         vec_cols = const.tile([P, P], F32)
         nc.vector.tensor_copy(out=vec_cols[:], in_=vec_bank[:])
 
-        interleave_next()
-        interleave_next()
+        stats = start_pool.tile([P, TOKEN_TILES, D_MODEL // BN_STATS_MAX, BN_STATS_OUT], F32)
+        mean_var = start_pool.tile([P, TOKEN_TILES, 2], F32)
+        for i in range(TOKEN_TILES):
+            for part in range(D_MODEL // BN_STATS_MAX):
+                nc.vector.bn_stats(
+                    out=stats[:, i, part, :], in_=x_sb[:, i, part * BN_STATS_MAX : (part + 1) * BN_STATS_MAX]
+                )
+            nc.vector.bn_aggr(out=mean_var[:, i, :], in_=stats[:, i, :, :].rearrange("p a b -> p (a b)"))
+        var_eps = start_pool.tile([P, TOKEN_TILES], F32)
+        nc.vector.tensor_scalar(out=var_eps[:], in0=mean_var[:, :, 1], scalar1=EPS, scalar2=None, op0=ALU.add)
         std = start_pool.tile([P, TOKEN_TILES], F32)
         nc.scalar.activation(out=std[:], in_=var_eps[:], func=ACT.Sqrt)
         rstd = start_pool.tile([P, TOKEN_TILES], F32)
@@ -222,7 +224,6 @@ def tile_transformerlayershard_pb_kernel(
         nc.vector.scalar_tensor_tensor(
             out=minus_mean_rstd[:], in0=mean_var[:, :, 0], scalar=-1.0, in1=rstd[:], op0=ALU.mult, op1=ALU.mult
         )
-        interleave_next()
         z = start_pool.tile([P, TOKEN_TILES, D_MODEL], F32)
         for i in range(TOKEN_TILES):
             gain = rstd[:, i : i + 1]
@@ -233,9 +234,6 @@ def tile_transformerlayershard_pb_kernel(
                 nc.vector.tensor_scalar(
                     out=z[:, i, :], in0=x_sb[:, i, :], scalar1=gain, scalar2=shift, op0=ALU.mult, op1=ALU.add
                 )
-        interleave_next()
-        quantise_next()
-        quantise_next()
 
         xn_rows = start_pool.tile([P, D_PASSES, PACK, TOKENS], BF16)
         xn_grouped = start_pool.tile([P, D_PASSES, TOKENS, PACK], BF16, align_bytes=64)
@@ -257,7 +255,6 @@ def tile_transformerlayershard_pb_kernel(
                         out=xn_rows[:, c, t, :], in0=z_bank[:], scalar1=gain, scalar2=shift, op0=ALU.mult, op1=ALU.add
                     )
             interleave(nc, xn_grouped[:, c], xn_rows[:, c], VECTOR_COLS_BESIDE_GELU)
-        quantise_next()
         for c in range(D_PASSES):
             quantise(nc, xn_codes[:, c, :], xn_scales[:, c, :], xn_grouped[:, c])
 
@@ -268,25 +265,26 @@ def tile_transformerlayershard_pb_kernel(
             for pair in range(TOKEN_TILES // 2):
                 attn_bank = work_banks.tile([P, 2, 2 * P], F32, tag="work")
                 for u in range(2):
-                    for n in range(2):
-                        first_word = 256 * c + P * u
+                    for m in range(2):
+                        first_word = (2 * c + u) * P
                         nc.tensor.transpose(
-                            attn_bank[:, u, n * P : (n + 1) * P],
-                            attn_words[:, 2 * pair + n, first_word : first_word + P],
+                            attn_bank[:, u, m * P : (m + 1) * P],
+                            attn_words[:, 2 * pair + m, first_word : first_word + P],
                             ident_f32[:],
                         )
                 nc.scalar.copy(
                     out=grouped_words[:, c, 2 * P * pair : 2 * P * (pair + 1), :],
                     in_=attn_bank[:].rearrange("p u s -> p s u"),
                 )
-        while len(interleaved) < INTERLEAVED_AHEAD:
-            interleave_next()
         for c in range(D_PASSES):
             nc.vector.quantize_mx(
                 out=attn_codes[:, c, :].bitcast(FP8X4),
                 scales=attn_scales[:, c, :],
                 in_=attn_grouped[:, c * TOKENS * PACK : (c + 1) * TOKENS * PACK],
             )
+
+        while len(interleaved) < INTERLEAVED_AHEAD:
+            interleave_next()
         while len(quantised) < QUANTISED_AHEAD:
             quantise_next()
 
@@ -327,14 +325,14 @@ def tile_transformerlayershard_pb_kernel(
             nc.sync.dma_start(out=out_rows[i * P : (i + 1) * P, cols], in_=result[:])
 
         first_acc = [acc_banks.tile([P, BANK], F32, name="acc%d" % i, tag="acc") for i in range(TOKEN_TILES)]
-        h_rows_of = {}
+        h_rows = None
         for s in range(FF_PASSES + SECOND_LAG):
-            g = s - 1
-            if g in h_rows_of:
+            h_waits = 1 <= s <= FF_PASSES
+            if h_waits:
                 h_grouped = h_pool.tile([P, TOKENS, PACK], BF16, align_bytes=64)
-                interleave(nc, h_grouped, h_rows_of[g], TOKENS)
+                interleave(nc, h_grouped, h_rows, TOKENS)
             if s < FF_PASSES:
-                h_rows_of[s] = first_product(s)
+                h_rows = first_product(s)
                 for c in range(D_PASSES):
                     prepare_next()
             if s == SECOND_LAG:
@@ -344,18 +342,18 @@ def tile_transformerlayershard_pb_kernel(
             if s >= SECOND_LAG:
                 second_product(first_acc, s - SECOND_LAG)
                 prepare_next()
-            if g in h_rows_of:
-                quantise(nc, h_codes[:, g, :], h_scales[:, g, :], h_grouped[:])
+            if h_waits:
+                quantise(nc, h_codes[:, s - 1, :], h_scales[:, s - 1, :], h_grouped[:])
 
         second_acc = [work_banks.tile([P, BANK], F32, name="acc%d" % i, tag="work") for i in range(TOKEN_TILES)]
         rounds = D_PASSES + FF_PASSES
-        for n in range(rounds):
-            if n < D_PASSES:
-                attention_pass(second_acc, n)
+        for r in range(rounds):
+            if r < D_PASSES:
+                attention_pass(second_acc, r)
             else:
-                second_product(second_acc, n - D_PASSES)
+                second_product(second_acc, r - D_PASSES)
             prepare_next()
-            if n >= rounds - TOKEN_TILES:
-                add_b2_and_store(first_acc, n - (rounds - TOKEN_TILES), halves[0])
+            if r >= rounds - TOKEN_TILES:
+                add_b2_and_store(first_acc, r - (rounds - TOKEN_TILES), halves[0])
         for i in range(TOKEN_TILES):
             add_b2_and_store(second_acc, i, halves[1])

from contextlib import ExitStack

import concourse.mybir as mybir
from concourse.masks import make_identity

BF16 = mybir.dt.bfloat16
F32 = mybir.dt.float32
U32 = mybir.dt.uint32
U8 = mybir.dt.uint8
FP8X4 = mybir.dt.float8_e4m3fn_x4
ACT = mybir.ActivationFunctionType
ALU = mybir.AluOpType

P = 128
PACK = 4
K_PASS = P * PACK
BANK = 512
BANKS = 8
BN_STATS_MAX = 512
BN_STATS_OUT = 6

TOKENS = 512
D_MODEL = 1024
D_FF = 4096
EPS = 1e-5
TOKEN_TILES = TOKENS // P
D_PASSES = D_MODEL // K_PASS
FF_PASSES = D_FF // K_PASS

SECOND_LAG = 4

INTERLEAVED_AHEAD = 6
QUANTISED_AHEAD = 3
RAW_BUFS = 10
GROUPED_BUFS = INTERLEAVED_AHEAD - QUANTISED_AHEAD + 3
CODES_BUFS = QUANTISED_AHEAD + 5

VECTOR_COLS_BESIDE_GELU = 320
VECTOR_COLS_AFTER_GELU = 224

B1_AT = 0
LN_SCALE_AT = 32
LN_OFFSET_AT = 64

FLOPS = 2 * TOKENS * (D_MODEL * D_MODEL + 2 * D_MODEL * D_FF)


def rows_128_apart(w, first_row, cols):
    return [w[first_row : first_row + K_PASS, cols].rearrange("(t p) n -> p t n", p=P)]


def rows_in_pairs(w, first_row, cols):
    return [
        w[first_row + 2 * P * u : first_row + 2 * P * (u + 1), cols].rearrange("(p e) n -> p e n", e=2)
        for u in range(2)
    ]


def interleave(nc, grouped, rows, vector_cols):
    width = rows.shape[2]
    nc.vector.tensor_copy(
        out=grouped[:, 0:vector_cols, :].rearrange("p (c i) t -> p c t i", i=4),
        in_=rows[:, :, 0:vector_cols].rearrange("p t (c i) -> p c t i", i=4),
    )
    if vector_cols < width:
        nc.scalar.copy(
            out=grouped[:, vector_cols:width, :].rearrange("p (c i) t -> p c t i", i=4),
            in_=rows[:, :, vector_cols:width].rearrange("p t (c i) -> p c t i", i=4),
        )


def quantise(nc, codes, scales, grouped):
    nc.vector.quantize_mx(
        out=codes.bitcast(FP8X4), scales=scales, in_=grouped.rearrange("p w t -> p (w t)")
    )


def add_pass_to_out(nc, acc, act_codes, act_scales, weight, start, stop):
    w_codes, w_scales = weight
    for i in range(TOKEN_TILES):
        tokens = slice(i * P, (i + 1) * P)
        nc.tensor.matmul_mx(
            out=acc[i][:],
            lhsT=act_codes[:, tokens].bitcast(FP8X4),
            lhsT_scale=act_scales[:, tokens],
            rhs=w_codes[:].bitcast(FP8X4),
            rhs_scale=w_scales[:],
            start=start,
            stop=stop,
        )


def tile_transformerlayershard_pb_kernel(
    tc, x, attn_vec, ln_scale, ln_offset, Wo, W1, b1, W2, b2, out
):
    nc = tc.nc
    x_rows = x.rearrange("o s d -> (o s) d")
    out_rows = out.rearrange("o s d -> (o s) d")
    halves = [slice(0, BANK), slice(BANK, 2 * BANK)]

    with ExitStack() as ctx:
        const = ctx.enter_context(tc.tile_pool(name="const", bufs=1))
        keep = ctx.enter_context(tc.tile_pool(name="keep", bufs=1))
        start_pool = ctx.enter_context(tc.tile_pool(name="start", bufs=1))
        raw_pool = ctx.enter_context(tc.tile_pool(name="raw", bufs=RAW_BUFS))
        grouped_pool = ctx.enter_context(tc.tile_pool(name="grouped", bufs=GROUPED_BUFS))
        codes_pool = ctx.enter_context(tc.tile_pool(name="codes", bufs=CODES_BUFS))
        h_pool = ctx.enter_context(tc.tile_pool(name="h", bufs=2))
        out_pool = ctx.enter_context(tc.tile_pool(name="out", bufs=2 * TOKEN_TILES))
        acc_banks = ctx.enter_context(tc.psum_pool(name="acc_banks", bufs=BANKS // 2))
        work_banks = ctx.enter_context(tc.psum_pool(name="work_banks", bufs=BANKS // 2))

        xn_codes = keep.tile([P, D_PASSES, TOKENS], U32, align_bytes=64)
        xn_scales = keep.tile([P, D_PASSES, TOKENS], U8, align_bytes=64)
        attn_codes = keep.tile([P, D_PASSES, TOKENS], U32, align_bytes=64)
        attn_scales = keep.tile([P, D_PASSES, TOKENS], U8, align_bytes=64)
        h_codes = keep.tile([P, FF_PASSES, TOKENS], U32, align_bytes=64)
        h_scales = keep.tile([P, FF_PASSES, TOKENS], U8, align_bytes=64)

        blocks = []
        for s in range(FF_PASSES + SECOND_LAG):
            vector_cols = VECTOR_COLS_BESIDE_GELU if s < FF_PASSES else VECTOR_COLS_AFTER_GELU
            if s < FF_PASSES:
                for c in range(D_PASSES):
                    blocks.append((rows_128_apart(W1, c * K_PASS, slice(s * BANK, (s + 1) * BANK)), vector_cols))
            if s == SECOND_LAG:
                for c in range(D_PASSES):
                    blocks.append((rows_in_pairs(Wo, c * K_PASS, halves[0]), vector_cols))
            if s >= SECOND_LAG:
                blocks.append((rows_128_apart(W2, (s - SECOND_LAG) * K_PASS, halves[0]), vector_cols))
        for c in range(D_PASSES):
            blocks.append((rows_in_pairs(Wo, c * K_PASS, halves[1]), VECTOR_COLS_AFTER_GELU))
        for g in range(FF_PASSES):
            blocks.append((rows_128_apart(W2, g * K_PASS, halves[1]), VECTOR_COLS_AFTER_GELU))

        loaded = []
        interleaved = []
        quantised = []
        used = []

        def load_next():
            if len(loaded) < len(blocks):
                pieces = blocks[len(loaded)][0]
                raw = raw_pool.tile([P, PACK, BANK], BF16)
                rows_each = PACK // len(pieces)
                for k, piece in enumerate(pieces):
                    nc.sync.dma_start(out=raw[:, k * rows_each : (k + 1) * rows_each, :], in_=piece)
                loaded.append(raw)

        def interleave_next():
            if len(interleaved) < len(blocks):
                n = len(interleaved)
                grouped = grouped_pool.tile([P, BANK, PACK], BF16, align_bytes=64)
                interleave(nc, grouped, loaded[n], blocks[n][1])
                interleaved.append(grouped)
                load_next()

        def quantise_next():
            if len(quantised) < len(blocks):
                codes = codes_pool.tile([P, BANK], U32, align_bytes=64)
                scales = codes_pool.tile([P, BANK], U8, align_bytes=64)
                quantise(nc, codes[:], scales[:], interleaved[len(quantised)][:])
                quantised.append((codes, scales))

        def prepare_next():
            interleave_next()
            quantise_next()

        def next_block():
            used.append(quantised[len(used)])
            return used[len(used) - 1]

        one = const.tile([P, 1], F32)
        nc.vector.memset(one[:], 1.0)
        vec_rows = const.tile([P, P], BF16)
        nc.vector.memset(vec_rows[:], 0.0)
        table_warmer = const.tile([P, 1], F32)
        nc.scalar.activation(out=table_warmer[:], in_=one[:], func=ACT.Sqrt)
        ident_f32 = const.tile([P, P], F32)
        make_identity(nc, ident_f32[:])
        ident_bf16 = const.tile([P, P], BF16)
        make_identity(nc, ident_bf16[:])

        x_sb = start_pool.tile([P, TOKEN_TILES, D_MODEL], BF16)
        for i in range(TOKEN_TILES):
            nc.sync.dma_start(out=x_sb[:, i, :], in_=x_rows[i * P : (i + 1) * P, :])
        for c in range(D_PASSES):
            load_next()
        for vec, at in ((b1, B1_AT), (ln_scale, LN_SCALE_AT), (ln_offset, LN_OFFSET_AT)):
            vec_as_rows = vec.rearrange("(r c) -> r c", c=P)
            nc.sync.dma_start(out=vec_rows[at : at + vec_as_rows.shape[0], :], in_=vec_as_rows)
        for c in range(D_PASSES):
            load_next()
        attn_sb = start_pool.tile([P, TOKEN_TILES * D_MODEL], BF16)
        nc.sync.dma_start(
            out=attn_sb[:].rearrange("p (i e) -> p i e", i=TOKEN_TILES),
            in_=attn_vec.rearrange("(i p) e -> p i e", p=P),
        )
        while len(loaded) < RAW_BUFS:
            load_next()
        b2_all = const.tile([P, D_MODEL], BF16)
        nc.sync.dma_start(out=b2_all[:], in_=b2.partition_broadcast(P))

        vec_bank = work_banks.tile([P, P], BF16, tag="work")
        nc.tensor.transpose(vec_bank[:], vec_rows[:], ident_bf16[:])
        vec_cols = const.tile([P, P], F32)
        nc.vector.tensor_copy(out=vec_cols[:], in_=vec_bank[:])

        stats = start_pool.tile([P, TOKEN_TILES, D_MODEL // BN_STATS_MAX, BN_STATS_OUT], F32)
        mean_var = start_pool.tile([P, TOKEN_TILES, 2], F32)
        for i in range(TOKEN_TILES):
            for part in range(D_MODEL // BN_STATS_MAX):
                nc.vector.bn_stats(
                    out=stats[:, i, part, :], in_=x_sb[:, i, part * BN_STATS_MAX : (part + 1) * BN_STATS_MAX]
                )
            nc.vector.bn_aggr(out=mean_var[:, i, :], in_=stats[:, i, :, :].rearrange("p a b -> p (a b)"))
        var_eps = start_pool.tile([P, TOKEN_TILES], F32)
        nc.vector.tensor_scalar(out=var_eps[:], in0=mean_var[:, :, 1], scalar1=EPS, scalar2=None, op0=ALU.add)
        std = start_pool.tile([P, TOKEN_TILES], F32)
        nc.scalar.activation(out=std[:], in_=var_eps[:], func=ACT.Sqrt)
        rstd = start_pool.tile([P, TOKEN_TILES], F32)
        nc.vector.reciprocal(out=rstd[:], in_=std[:])
        minus_mean_rstd = start_pool.tile([P, TOKEN_TILES], F32)
        nc.vector.scalar_tensor_tensor(
            out=minus_mean_rstd[:], in0=mean_var[:, :, 0], scalar=-1.0, in1=rstd[:], op0=ALU.mult, op1=ALU.mult
        )
        z = start_pool.tile([P, TOKEN_TILES, D_MODEL], F32)
        for i in range(TOKEN_TILES):
            gain = rstd[:, i : i + 1]
            shift = minus_mean_rstd[:, i : i + 1]
            if i % 2 == 0:
                nc.scalar.activation(out=z[:, i, :], in_=x_sb[:, i, :], func=ACT.Identity, bias=shift, scale=gain)
            else:
                nc.vector.tensor_scalar(
                    out=z[:, i, :], in0=x_sb[:, i, :], scalar1=gain, scalar2=shift, op0=ALU.mult, op1=ALU.add
                )

        xn_rows = start_pool.tile([P, D_PASSES, PACK, TOKENS], BF16)
        xn_grouped = start_pool.tile([P, D_PASSES, TOKENS, PACK], BF16, align_bytes=64)
        for c in range(D_PASSES):
            for t in range(PACK):
                j = c * PACK + t
                if c == 0:
                    z_bank = work_banks.tile([P, TOKENS], F32, tag="work")
                else:
                    z_bank = acc_banks.tile([P, TOKENS], F32, tag="acc")
                for i in range(TOKEN_TILES):
                    nc.tensor.transpose(z_bank[:, i * P : (i + 1) * P], z[:, i, j * P : (j + 1) * P], ident_f32[:])
                gain = vec_cols[:, LN_SCALE_AT + j : LN_SCALE_AT + j + 1]
                shift = vec_cols[:, LN_OFFSET_AT + j : LN_OFFSET_AT + j + 1]
                if t % 2 == 0:
                    nc.scalar.activation(out=xn_rows[:, c, t, :], in_=z_bank[:], func=ACT.Identity, bias=shift, scale=gain)
                else:
                    nc.vector.tensor_scalar(
                        out=xn_rows[:, c, t, :], in0=z_bank[:], scalar1=gain, scalar2=shift, op0=ALU.mult, op1=ALU.add
                    )
            interleave(nc, xn_grouped[:, c], xn_rows[:, c], VECTOR_COLS_BESIDE_GELU)
        for c in range(D_PASSES):
            quantise(nc, xn_codes[:, c, :], xn_scales[:, c, :], xn_grouped[:, c])

        attn_words = attn_sb[:].bitcast(F32).rearrange("p (i w) -> p i w", i=TOKEN_TILES)
        attn_grouped = start_pool.tile([P, D_PASSES * TOKENS * PACK], BF16, align_bytes=64)
        grouped_words = attn_grouped[:].bitcast(F32).rearrange("p (c s u) -> p c s u", c=D_PASSES, u=2)
        for c in range(D_PASSES):
            for pair in range(TOKEN_TILES // 2):
                attn_bank = work_banks.tile([P, 2, 2 * P], F32, tag="work")
                for u in range(2):
                    for m in range(2):
                        first_word = (2 * c + u) * P
                        nc.tensor.transpose(
                            attn_bank[:, u, m * P : (m + 1) * P],
                            attn_words[:, 2 * pair + m, first_word : first_word + P],
                            ident_f32[:],
                        )
                nc.scalar.copy(
                    out=grouped_words[:, c, 2 * P * pair : 2 * P * (pair + 1), :],
                    in_=attn_bank[:].rearrange("p u s -> p s u"),
                )
        for c in range(D_PASSES):
            nc.vector.quantize_mx(
                out=attn_codes[:, c, :].bitcast(FP8X4),
                scales=attn_scales[:, c, :],
                in_=attn_grouped[:, c * TOKENS * PACK : (c + 1) * TOKENS * PACK],
            )

        while len(interleaved) < INTERLEAVED_AHEAD:
            interleave_next()
        while len(quantised) < QUANTISED_AHEAD:
            quantise_next()

        def first_product(g):
            w1 = [next_block() for c in range(D_PASSES)]
            h_rows = h_pool.tile([P, PACK, TOKENS], BF16)
            for t in range(PACK):
                cols = slice(t * P, (t + 1) * P)
                h_bank = work_banks.tile([P, TOKENS], F32, tag="work")
                for c, (codes, scales) in enumerate(w1):
                    nc.tensor.matmul_mx(
                        out=h_bank[:],
                        lhsT=codes[:, cols].bitcast(FP8X4),
                        lhsT_scale=scales[:, cols],
                        rhs=xn_codes[:, c, :].bitcast(FP8X4),
                        rhs_scale=xn_scales[:, c, :],
                        start=(c == 0),
                        stop=(c == D_PASSES - 1),
                    )
                j = g * PACK + t
                nc.scalar.activation(
                    out=h_rows[:, t, :],
                    in_=h_bank[:],
                    func=ACT.Gelu_apprx_tanh,
                    bias=vec_cols[:, B1_AT + j : B1_AT + j + 1],
                )
            return h_rows

        def attention_pass(acc, c):
            add_pass_to_out(nc, acc, attn_codes[:, c, :], attn_scales[:, c, :], next_block(), c == 0, False)

        def second_product(acc, g):
            add_pass_to_out(nc, acc, h_codes[:, g, :], h_scales[:, g, :], next_block(), False, g == FF_PASSES - 1)

        def add_b2_and_store(acc, i, cols):
            result = out_pool.tile([P, BANK], F32)
            nc.vector.tensor_tensor(out=result[:], in0=acc[i][:], in1=b2_all[:, cols], op=ALU.add)
            nc.sync.dma_start(out=out_rows[i * P : (i + 1) * P, cols], in_=result[:])

        first_acc = [acc_banks.tile([P, BANK], F32, name="acc%d" % i, tag="acc") for i in range(TOKEN_TILES)]
        h_rows = None
        for s in range(FF_PASSES + SECOND_LAG):
            h_waits = 1 <= s <= FF_PASSES
            if h_waits:
                h_grouped = h_pool.tile([P, TOKENS, PACK], BF16, align_bytes=64)
                interleave(nc, h_grouped, h_rows, TOKENS)
            if s < FF_PASSES:
                h_rows = first_product(s)
                for c in range(D_PASSES):
                    prepare_next()
            if s == SECOND_LAG:
                for c in range(D_PASSES):
                    attention_pass(first_acc, c)
                    prepare_next()
            if s >= SECOND_LAG:
                second_product(first_acc, s - SECOND_LAG)
                prepare_next()
            if h_waits:
                quantise(nc, h_codes[:, s - 1, :], h_scales[:, s - 1, :], h_grouped[:])

        second_acc = [work_banks.tile([P, BANK], F32, name="acc%d" % i, tag="work") for i in range(TOKEN_TILES)]
        rounds = D_PASSES + FF_PASSES
        for r in range(rounds):
            if r < D_PASSES:
                attention_pass(second_acc, r)
            else:
                second_product(second_acc, r - D_PASSES)
            prepare_next()
            if r >= rounds - TOKEN_TILES:
                add_b2_and_store(first_acc, r - (rounds - TOKEN_TILES), halves[0])
        for i in range(TOKEN_TILES):
            add_b2_and_store(second_acc, i, halves[1])
